import numpy as np
import ml_dtypes


def mxq(x, axis, fmt="e4m3"):
    dtype, down = {"e4m3": (ml_dtypes.float8_e4m3fn, 7), "e5m2": (ml_dtypes.float8_e5m2, 14)}[fmt]
    v = np.moveaxis(np.asarray(x, np.float32).astype(ml_dtypes.bfloat16).astype(np.float64), axis, -1)
    blocks = v.reshape(v.shape[:-1] + (-1, 32))
    amax = np.abs(blocks).max(-1, keepdims=True)
    byte = np.maximum(np.where(amax > 0, np.frexp(amax)[1] - 1 + 127, 0) - down, 1)
    scale = np.exp2(byte - 127.0)
    codes = (blocks / scale).astype(np.float32).astype(dtype).astype(np.float64)
    return np.moveaxis((codes * scale).reshape(v.shape), -1, axis)


WIDE = False


def mx_kscale(k):
    if not WIDE:
        return np.ones(k)
    levels = np.array([10, -10, 5, -5, 0])
    if k % 512:
        return np.exp2(np.random.permutation(np.resize(levels, k // 32))).repeat(32)
    a = np.empty((k // 512, 16))
    for p in range(k // 512):
        a[p, :8] = np.random.permutation(np.resize(levels, 8))
        for g in range(8):
            far = levels[np.abs(levels - a[p, g]) >= 10]
            a[p, g + 8] = far[np.random.randint(len(far))]
    return np.exp2(a.ravel()).repeat(32)


BF16 = ml_dtypes.bfloat16


def bf(x):
    return np.asarray(x, np.float32).astype(BF16)


def f64(x):
    return np.asarray(x).astype(np.float64)


B, T, H, KV, D = 1, 512, 16, 4, 128
G = H // KV
NEG = -1e9


def setup_inputs():
    s = mx_kscale(T)
    keep = np.random.random((1, 1, T, T)) < 0.5
    mask_w = np.where(keep, 1.0 + 0.3 * np.random.standard_normal((1, 1, T, T)), 0.0)
    mask_b = np.where(keep, 0.5 * np.random.standard_normal((1, 1, T, T)) + np.log(s)[None, None, None, :], NEG)
    return {"q_rot": bf(np.random.standard_normal((B, T, H, D))),
            "k_rot": bf(np.random.standard_normal((B, T, KV, D))),
            "v": bf(np.random.standard_normal((B, T, KV, D)) * 2.0 * (s.max() / s)[None, :, None, None]),
            "mask_w": bf(mask_w), "mask_b": bf(mask_b)}


def reference(q_rot, k_rot, v, mask_w, mask_b):
    qg = f64(q_rot).transpose(0, 2, 1, 3).reshape(B, KV, G * T, D)
    kt = f64(k_rot).transpose(0, 2, 3, 1)
    s = (qg @ kt).reshape(B, H, T, T) * (1.0 / np.sqrt(D))
    s = s * f64(mask_w) + f64(mask_b)
    e = np.exp(s - s.max(-1, keepdims=True))
    eq = mxq(e.reshape(B, KV, G * T, T), 3, "e4m3")
    vq = mxq(f64(v).transpose(0, 2, 1, 3), 2, "e4m3")
    o = (eq @ vq).reshape(B, H, T, D) / e.sum(-1, keepdims=True)
    return o.transpose(0, 2, 1, 3)

@@ -1,0 +1,338 @@
+from contextlib import ExitStack
+import math
+
+import concourse.mybir as mybir
+from concourse.masks import make_identity
+
+BF16 = mybir.dt.bfloat16
+F32 = mybir.dt.float32
+U32 = mybir.dt.uint32
+U8 = mybir.dt.uint8
+FP8X4 = mybir.dt.float8_e4m3fn_x4
+ALU = mybir.AluOpType
+ACT = mybir.ActivationFunctionType
+AXIS = mybir.AxisListType
+
+P = 128
+T = 512
+H = 16
+KV = 4
+D = 128
+G = H // KV
+QT = T // P
+PACK = 4
+HALF = T // 2
+NG = QT * KV
+PAIRED = 14
+HALVED = 1
+SCALE = 1.0 / math.sqrt(D)
+
+FLOPS = 2 * 2 * H * T * T * D
+
+
+def tile_mistralselfattention_pb_kernel(tc, q_rot, k_rot, v, mask_w, mask_b, out):
+    nc = tc.nc
+
+    q_view = q_rot.rearrange("b (qt p) h d -> p (b qt) h d", p=P)
+    k_view = k_rot.rearrange("b (kt p) kv d -> p (b kt) kv d", p=P)
+    mw_view = mask_w.rearrange("a b (qt p) k -> p (a b qt) k", p=P)
+    mb_view = mask_b.rearrange("a b (qt p) k -> p (a b qt) k", p=P)
+    out_view = out.rearrange("b (qt p) h d -> p (b qt) h d", p=P)
+    v_view = v.rearrange("b (p t) kv d -> p (b t) (kv d)", t=PACK)
+
+    units = []
+    for g in range(NG):
+        heads = G // 2 if g >= NG - HALVED else G
+        for first in range(0, G, heads):
+            units.append((g // KV, g % KV, first, heads))
+    n_units = len(units)
+
+    with ExitStack() as ctx:
+        keep = ctx.enter_context(tc.tile_pool(name="keep", bufs=1))
+        work = ctx.enter_context(tc.tile_pool(name="work", bufs=3))
+        ps_scores = ctx.enter_context(tc.psum_pool(name="ps_scores", bufs=G))
+        ps_e = ctx.enter_context(tc.psum_pool(name="ps_e", bufs=2))
+        ps_q = ctx.enter_context(tc.psum_pool(name="ps_q", bufs=1))
+        ps_out = ctx.enter_context(tc.psum_pool(name="ps_out", bufs=1))
+        ctx.enter_context(tc.manual_schedule())
+
+        k_sb = [keep.tile([P, QT, D], BF16, name="k_sb%d" % kv) for kv in range(KV)]
+        q_sb = [keep.tile([P, G, D], BF16, name="q_sb%d" % g) for g in range(NG)]
+        mw_sb = [keep.tile([P, T], BF16, name="mw_sb%d" % qt) for qt in range(QT)]
+        mb_sb = [keep.tile([P, T], BF16, name="mb_sb%d" % qt) for qt in range(QT)]
+        v_sb = keep.tile([P, PACK, KV * D], BF16)
+        for g in range(NG):
+            qt, kv = divmod(g, KV)
+            if qt == 0:
+                nc.sync.dma_start(out=k_sb[kv][:], in_=k_view[:, :, kv, :])
+            nc.sync.dma_start(out=q_sb[g][:], in_=q_view[:, qt, kv * G : (kv + 1) * G, :])
+            if kv == 0:
+                nc.sync.dma_start(out=mw_sb[qt][:], in_=mw_view[:, qt])
+                nc.sync.dma_start(out=mb_sb[qt][:], in_=mb_view[:, qt])
+            if g == 0:
+                nc.sync.dma_start(out=v_sb[:], in_=v_view)
+
+        zeros = keep.tile([P, P], BF16)
+        nc.vector.memset(zeros[:], 0.0)
+        for i in range(5):
+            dummy = ps_scores.tile([P, 4, P], F32, tag="s_ps")
+            nc.tensor.matmul(
+                dummy[:], lhsT=zeros[:], rhs=zeros[:].unsqueeze(1).to_broadcast([P, 4, P]), start=True, stop=True
+            )
+        ident_bf = keep.tile([P, P], BF16)
+        make_identity(nc, ident_bf[:])
+        ident_f32 = keep.tile([P, P], F32)
+        make_identity(nc, ident_f32[:])
+        warm = keep.tile([P, 1], F32)
+        nc.vector.memset(warm[:], 0.0)
+        nc.scalar.activation(out=warm[:], in_=warm[:], func=ACT.Exp)
+
+        kT = keep.tile([P, KV, T], BF16)
+        v_grouped = keep.tile([P, KV * D, PACK], BF16, align_bytes=64)
+        v_codes = keep.tile([P, KV * D], U32, align_bytes=64)
+        v_scales = keep.tile([P, KV * D], U8, align_bytes=64)
+
+        tiles = {}
+
+        def turn_keys(kv):
+            kT_ps = ps_e.tile([P, QT, P], BF16, tag="eT_ps")
+            for kt in range(QT):
+                nc.tensor.transpose(kT_ps[:, kt, :], k_sb[kv][:, kt, :], ident_bf[:])
+            tiles["kT_ps", kv] = kT_ps
+
+        def copy_keys(kv):
+            nc.scalar.copy(out=kT[:, kv, :], in_=tiles["kT_ps", kv][:].rearrange("d kt p -> d (kt p)"))
+
+        def turn_queries(u, lo=0, hi=None):
+            qt, kv, first, heads = units[u]
+            if lo == 0:
+                tiles["qT_ps", u] = ps_q.tile([P, G, P], BF16, name="qT_ps")
+                tiles["qT", u] = work.tile([P, G, P], BF16, name="qT")
+            for i in range(lo, heads if hi is None else hi):
+                nc.tensor.transpose(tiles["qT_ps", u][:, i, :], q_sb[qt * KV + kv][:, first + i, :], ident_bf[:])
+
+        def copy_queries(u, lo=0, hi=None, eng=None):
+            hi = units[u][3] if hi is None else hi
+            if eng == "V":
+                nc.vector.tensor_copy(out=tiles["qT", u][:, lo:hi], in_=tiles["qT_ps", u][:, lo:hi])
+            else:
+                nc.scalar.copy(out=tiles["qT", u][:, lo:hi], in_=tiles["qT_ps", u][:, lo:hi])
+
+        def scores_matmul(u, lo=0, hi=None):
+            qt, kv, first, heads = units[u]
+            for i in range(lo, heads if hi is None else hi):
+                s_ps = ps_scores.tile([P, T], F32, tag="s_ps")
+                nc.tensor.matmul(
+                    s_ps[:], lhsT=tiles["qT", u][:, i, :], rhs=kT[:, kv, :], start=True, stop=True
+                )
+                tiles["s_ps", u, i] = s_ps
+
+        def weigh_scores(u, lo=0, hi=None):
+            qt, kv, first, heads = units[u]
+            if lo == 0:
+                tiles["s2", u] = work.tile([P, G, T], F32, bufs=4, name="s2")
+            for i in range(lo, heads if hi is None else hi):
+                nc.vector.scalar_tensor_tensor(
+                    out=tiles["s2", u][:, i, :], in0=tiles["s_ps", u, i][:], scalar=SCALE, in1=mw_sb[qt][:],
+                    op0=ALU.mult, op1=ALU.mult,
+                )
+
+        def add_bias(u, lo=0, hi=None, eng=None):
+            qt, kv, first, heads = units[u]
+            hi = heads if hi is None else hi
+            s2 = tiles["s2", u][:, lo:hi]
+            if eng == "V":
+                for i in range(lo, hi):
+                    nc.vector.tensor_tensor(out=tiles["s2", u][:, i, :], in0=tiles["s2", u][:, i, :], in1=mb_sb[qt][:], op=ALU.add)
+            else:
+                nc.gpsimd.tensor_tensor(
+                    out=s2, in0=s2, in1=mb_sb[qt][:].unsqueeze(1).to_broadcast([P, hi - lo, T]), op=ALU.add
+                )
+
+        def row_maxima(u, lo=0, hi=None, step=1):
+            if lo == 0:
+                tiles["neg_max", u] = work.tile([P, G], F32, name="neg_max")
+            for i in range(lo, units[u][3] if hi is None else hi, step):
+                nc.vector.tensor_reduce(
+                    out=tiles["neg_max", u][:, i : i + step], in_=tiles["s2", u][:, i : i + step, :], axis=AXIS.X,
+                    op=ALU.max, negate=True,
+                )
+
+        def exponentials(u, lo=0, hi=None):
+            if lo == 0:
+                tiles["e_sb", u] = work.tile([P, G, T], BF16, name="e_sb")
+                if u >= PAIRED or u % 2 == 0:
+                    sums = work.tile([P, 2, G], F32, bufs=4, name="rowsum")
+                tiles["rowsum", u] = sums[:, 0] if u >= PAIRED or u % 2 == 0 else tiles["rowsums", u - 1][:, 1]
+                if u >= PAIRED or u % 2 == 0:
+                    tiles["rowsums", u] = sums
+            for i in range(lo, units[u][3] if hi is None else hi):
+                nc.scalar.activation(
+                    out=tiles["e_sb", u][:, i, :], in_=tiles["s2", u][:, i, :], func=ACT.Exp,
+                    bias=tiles["neg_max", u][:, i : i + 1], scale=1.0,
+                    accum_out=tiles["rowsum", u][:, i : i + 1],
+                )
+
+        def turn_e(u, lo=0, hi=None, spare=False):
+            hi = units[u][3] if hi is None else hi
+            for first in range(lo, hi, 2):
+                eT_ps = (ps_scores.tile([P, 2, 2, P], F32, name="eT_ps2", tag="s_ps") if spare else ps_e.tile([P, 2, 2, P], F32, tag="eT_ps"))
+                for j in range(min(2, hi - first)):
+                    e_words = tiles["e_sb", u][:, first + j, :].bitcast(F32)
+                    for half in range(2):
+                        nc.tensor.transpose(eT_ps[:, j, half, :], e_words[:, half::2], ident_f32[:])
+                tiles["eT_ps", u, first] = eT_ps
+
+        def group_e(u, lo=0, hi=None, eng=None):
+            if lo == 0:
+                tiles["e_grouped", u] = work.tile([P, G, P, PACK], BF16, align_bytes=64, name="e_grouped")
+            hi = units[u][3] if hi is None else hi
+            for first in range(lo, hi, 2):
+                w = min(2, hi - first)
+                args = dict(
+                    out=tiles["e_grouped", u][:, first : first + w].bitcast(F32),
+                    in_=tiles["eT_ps", u, first][:, :w].rearrange("p j half q -> p j q half"),
+                )
+                if eng == "V":
+                    nc.vector.tensor_copy(**args)
+                else:
+                    nc.scalar.copy(**args)
+
+        def quantise_e(u, lo=0, hi=None):
+            hi = units[u][3] if hi is None else hi
+            if lo == 0:
+                tiles["e_codes", u] = work.tile([P, G * P], U32, align_bytes=64, name="e_codes")
+                tiles["e_scales", u] = work.tile([P, G * P], U8, align_bytes=64, name="e_scales")
+                if u >= PAIRED or u % 2 == 0:
+                    inverse = work.tile([P, 2, G], F32, name="recip")
+                    tiles["inverse", u] = inverse
+                    tiles["recip", u] = inverse[:, 0]
+                else:
+                    tiles["recip", u] = tiles["inverse", u - 1][:, 1]
+            nc.vector.quantize_mx(
+                out=tiles["e_codes", u][:, lo * P : hi * P].bitcast(FP8X4),
+                scales=tiles["e_scales", u][:, lo * P : hi * P],
+                in_=tiles["e_grouped", u][:, lo:hi].rearrange("p i q t -> p (i q t)"),
+            )
+            if u >= PAIRED:
+                nc.vector.reciprocal(out=tiles["recip", u][:, lo:hi], in_=tiles["rowsum", u][:, lo:hi])
+            elif u % 2 == 0:
+                nc.vector.reciprocal(out=tiles["inverse", u][:], in_=tiles["rowsums", u][:])
+
+        def values_matmul(u, lo=0, hi=None, spare=False):
+            qt, kv, first, heads = units[u]
+            if lo == 0:
+                tiles["o_ps", u] = (ps_scores.tile([P, G, D], F32, name="o_ps", tag="s_ps") if spare else ps_out.tile([P, G, D], F32, name="o_ps"))
+            for i in range(lo, heads if hi is None else hi):
+                nc.tensor.matmul_mx(
+                    out=tiles["o_ps", u][:, i, :],
+                    lhsT=tiles["e_codes", u][:, i * P : (i + 1) * P].bitcast(FP8X4),
+                    lhsT_scale=tiles["e_scales", u][:, i * P : (i + 1) * P],
+                    rhs=v_codes[:, kv * D : (kv + 1) * D].bitcast(FP8X4),
+                    rhs_scale=v_scales[:, kv * D : (kv + 1) * D],
+                    start=True,
+                    stop=True,
+                )
+
+        def normalise(u, lo=0, hi=None, eng=None):
+            if lo == 0:
+                tiles["o_sb", u] = work.tile([P, G, D], F32, name="o_sb", bufs=5)
+            for i in range(lo, units[u][3] if hi is None else hi):
+                if eng == "V":
+                    nc.vector.tensor_scalar(
+                        out=tiles["o_sb", u][:, i, :], in0=tiles["o_ps", u][:, i, :],
+                        scalar1=tiles["recip", u][:, i : i + 1], scalar2=None, op0=ALU.mult,
+                    )
+                else:
+                    nc.scalar.activation(
+                        out=tiles["o_sb", u][:, i, :], in_=tiles["o_ps", u][:, i, :], func=ACT.Copy,
+                        scale=tiles["recip", u][:, i : i + 1],
+                    )
+
+        def store(u, lo=0, hi=None):
+            qt, kv, first, heads = units[u]
+            hi = heads if hi is None else hi
+            h0 = kv * G + first
+            nc.sync.dma_start(out=out_view[:, qt, h0 + lo : h0 + hi, :], in_=tiles["o_sb", u][:, lo:hi])
+
+        def run(stage, u, *more, **kw):
+            if 0 <= u < n_units:
+                stage(u, *more, **kw)
+
+        turn_queries(0, 0, 1)
+        turn_keys(0)
+        turn_queries(0, 1)
+        copy_queries(0, 0, 1, eng="V")
+        copy_keys(0)
+        copy_queries(0, 1, eng="V")
+        for k in range(-2, 14):
+            run(quantise_e, k - 2)
+            run(scores_matmul, k + 2)
+            run(values_matmul, k - 2)
+            if 0 < k + 3 < KV:
+                turn_keys(k + 3)
+            run(turn_queries, k + 3)
+            run(row_maxima, k, step=2)
+            run(exponentials, k)
+            run(turn_e, k)
+            run(normalise, k - 2)
+            run(store, k - 2)
+            if 0 < k + 3 < KV:
+                copy_keys(k + 3)
+            run(copy_queries, k + 3)
+            if k == -2:
+                nc.scalar.copy(out=v_grouped[:], in_=v_sb[:].rearrange("p t c -> p c t"))
+            run(group_e, k)
+            run(weigh_scores, k + 2)
+            if k + 2 == 0:
+                add_bias(0, 0, 1)
+                add_bias(0, 1, 2)
+                add_bias(0, 2)
+            else:
+                run(add_bias, k + 2)
+            if k == 0:
+                nc.vector.quantize_mx(
+                    out=v_codes[:].bitcast(FP8X4), scales=v_scales[:],
+                    in_=v_grouped[:].rearrange("p c t -> p (c t)"),
+                )
+        a, b, c = 14, 15, 16
+        quantise_e(a - 2)
+        scores_matmul(c)
+        values_matmul(a - 2)
+        row_maxima(a, 0, 2)
+        weigh_scores(c)
+        exponentials(a, 0, 2)
+        turn_e(a, 0, 2)
+        normalise(a - 2)
+        store(a - 2)
+        quantise_e(a - 1)
+        add_bias(c)
+        values_matmul(a - 1)
+        group_e(a, 0, 2)
+        row_maxima(a, 2)
+        exponentials(a, 2)
+        turn_e(a, 2)
+        row_maxima(b)
+        exponentials(b)
+        row_maxima(c)
+        exponentials(c)
+        turn_e(b)
+        normalise(a - 1)
+        store(a - 1)
+        turn_e(c, spare=True)
+        group_e(a, 2, eng="V")
+        quantise_e(a)
+        values_matmul(a, spare=True)
+        group_e(b, eng="V")
+        quantise_e(b)
+        values_matmul(b, spare=True)
+        group_e(c)
+        quantise_e(c)
+        values_matmul(c, spare=True)
+        normalise(a)
+        store(a)
+        normalise(b, eng="V")
+        store(b)
+        normalise(c, 0, 1)
+        normalise(c, 1, eng="V")
+        store(c)

@@ -69,12 +69,12 @@ def tile_mistralselfattention_pb_kernel(tc, q_rot, k_rot, v, mask_w, mask_b, out
             if kv == 0:
                 nc.sync.dma_start(out=mw_sb[qt][:], in_=mw_view[:, qt])
                 nc.sync.dma_start(out=mb_sb[qt][:], in_=mb_view[:, qt])
-            if g == 0:
+            if g == 1:
                 nc.sync.dma_start(out=v_sb[:], in_=v_view)
 
         zeros = keep.tile([P, P], BF16)
         nc.vector.memset(zeros[:], 0.0)
-        for i in range(5):
+        for i in range(4):
             dummy = ps_scores.tile([P, 4, P], F32, tag="s_ps")
             nc.tensor.matmul(
                 dummy[:], lhsT=zeros[:], rhs=zeros[:].unsqueeze(1).to_broadcast([P, 4, P]), start=True, stop=True
@@ -137,13 +137,20 @@ def tile_mistralselfattention_pb_kernel(tc, q_rot, k_rot, v, mask_w, mask_b, out
                     op0=ALU.mult, op1=ALU.mult,
                 )
 
+        def spread_bias(qt):
+            b_ps = ps_scores.tile([P, T], F32, name="b_ps", tag="s_ps")
+            nc.tensor.matmul(b_ps[:], lhsT=ident_bf[:], rhs=mb_sb[qt][:], start=True, stop=True)
+            tiles["b_ps", qt] = b_ps
+
         def add_bias(u, lo=0, hi=None, eng=None):
             qt, kv, first, heads = units[u]
             hi = heads if hi is None else hi
             s2 = tiles["s2", u][:, lo:hi]
             if eng == "V":
                 for i in range(lo, hi):
-                    nc.vector.tensor_tensor(out=tiles["s2", u][:, i, :], in0=tiles["s2", u][:, i, :], in1=mb_sb[qt][:], op=ALU.add)
+                    nc.vector.tensor_tensor(
+                        out=tiles["s2", u][:, i, :], in0=tiles["s2", u][:, i, :], in1=tiles["b_ps", qt][:], op=ALU.add
+                    )
             else:
                 nc.gpsimd.tensor_tensor(
                     out=s2, in0=s2, in1=mb_sb[qt][:].unsqueeze(1).to_broadcast([P, hi - lo, T]), op=ALU.add
@@ -265,7 +272,19 @@ def tile_mistralselfattention_pb_kernel(tc, q_rot, k_rot, v, mask_w, mask_b, out
         copy_queries(0, 0, 1, eng="V")
         copy_keys(0)
         copy_queries(0, 1, eng="V")
-        for k in range(-2, 14):
+        scores_matmul(0)
+        weigh_scores(0, 0, 1)
+        add_bias(0, 0, 1)
+        spread_bias(0)
+        turn_keys(1)
+        turn_queries(1)
+        copy_keys(1)
+        copy_queries(1)
+        nc.scalar.copy(out=v_grouped[:], in_=v_sb[:].rearrange("p t c -> p c t"))
+        weigh_scores(0, 1)
+        add_bias(0, 1, 3)
+        add_bias(0, 3, eng="V")
+        for k in range(-1, 14):
             run(quantise_e, k - 2)
             run(scores_matmul, k + 2)
             run(values_matmul, k - 2)
@@ -280,16 +299,9 @@ def tile_mistralselfattention_pb_kernel(tc, q_rot, k_rot, v, mask_w, mask_b, out
             if 0 < k + 3 < KV:
                 copy_keys(k + 3)
             run(copy_queries, k + 3)
-            if k == -2:
-                nc.scalar.copy(out=v_grouped[:], in_=v_sb[:].rearrange("p t c -> p c t"))
             run(group_e, k)
             run(weigh_scores, k + 2)
-            if k + 2 == 0:
-                add_bias(0, 0, 1)
-                add_bias(0, 1, 2)
-                add_bias(0, 2)
-            else:
-                run(add_bias, k + 2)
+            run(add_bias, k + 2)
             if k == 0:
                 nc.vector.quantize_mx(
                     out=v_codes[:].bitcast(FP8X4), scales=v_scales[:],

@@ -24,7 +24,6 @@ PACK = 4
 HALF = T // 2
 NG = QT * KV
 PAIRED = 14
-HALVED = 1
 SCALE = 1.0 / math.sqrt(D)
 
 FLOPS = 2 * 2 * H * T * T * D
@@ -40,12 +39,8 @@ def tile_mistralselfattention_pb_kernel(tc, q_rot, k_rot, v, mask_w, mask_b, out
     out_view = out.rearrange("b (qt p) h d -> p (b qt) h d", p=P)
     v_view = v.rearrange("b (p t) kv d -> p (b t) (kv d)", t=PACK)
 
-    units = []
-    for g in range(NG):
-        heads = G // 2 if g >= NG - HALVED else G
-        for first in range(0, G, heads):
-            units.append((g // KV, g % KV, first, heads))
-    n_units = len(units)
+    units = [(g // KV, g % KV, 0, G) for g in range(NG)]
+    n_units = NG
 
     with ExitStack() as ctx:
         keep = ctx.enter_context(tc.tile_pool(name="keep", bufs=1))
@@ -129,7 +124,7 @@ def tile_mistralselfattention_pb_kernel(tc, q_rot, k_rot, v, mask_w, mask_b, out
 
         def weigh_scores(u, lo=0, hi=None):
             qt, kv, first, heads = units[u]
-            if lo == 0:
+            if ("s2", u) not in tiles:
                 tiles["s2", u] = work.tile([P, G, T], F32, bufs=4, name="s2")
             for i in range(lo, heads if hi is None else hi):
                 nc.vector.scalar_tensor_tensor(
@@ -183,7 +178,10 @@ def tile_mistralselfattention_pb_kernel(tc, q_rot, k_rot, v, mask_w, mask_b, out
         def turn_e(u, lo=0, hi=None, spare=False):
             hi = units[u][3] if hi is None else hi
             for first in range(lo, hi, 2):
-                eT_ps = (ps_scores.tile([P, 2, 2, P], F32, name="eT_ps2", tag="s_ps") if spare else ps_e.tile([P, 2, 2, P], F32, tag="eT_ps"))
+                if spare:
+                    eT_ps = ps_scores.tile([P, 2, 2, P], F32, name="eT_ps2", tag="s_ps")
+                else:
+                    eT_ps = ps_e.tile([P, 2, 2, P], F32, tag="eT_ps")
                 for j in range(min(2, hi - first)):
                     e_words = tiles["e_sb", u][:, first + j, :].bitcast(F32)
                     for half in range(2):
@@ -191,7 +189,7 @@ def tile_mistralselfattention_pb_kernel(tc, q_rot, k_rot, v, mask_w, mask_b, out
                 tiles["eT_ps", u, first] = eT_ps
 
         def group_e(u, lo=0, hi=None, eng=None):
-            if lo == 0:
+            if ("e_grouped", u) not in tiles:
                 tiles["e_grouped", u] = work.tile([P, G, P, PACK], BF16, align_bytes=64, name="e_grouped")
             hi = units[u][3] if hi is None else hi
             for first in range(lo, hi, 2):
@@ -221,18 +219,23 @@ def tile_mistralselfattention_pb_kernel(tc, q_rot, k_rot, v, mask_w, mask_b, out
                 scales=tiles["e_scales", u][:, lo * P : hi * P],
                 in_=tiles["e_grouped", u][:, lo:hi].rearrange("p i q t -> p (i q t)"),
             )
+
+        def invert_sums(u):
             if u >= PAIRED:
-                nc.vector.reciprocal(out=tiles["recip", u][:, lo:hi], in_=tiles["rowsum", u][:, lo:hi])
+                nc.vector.reciprocal(out=tiles["recip", u], in_=tiles["rowsum", u])
             elif u % 2 == 0:
                 nc.vector.reciprocal(out=tiles["inverse", u][:], in_=tiles["rowsums", u][:])
 
         def values_matmul(u, lo=0, hi=None, spare=False):
             qt, kv, first, heads = units[u]
-            if lo == 0:
-                tiles["o_ps", u] = (ps_scores.tile([P, G, D], F32, name="o_ps", tag="s_ps") if spare else ps_out.tile([P, G, D], F32, name="o_ps"))
+            if spare:
+                o_ps = ps_scores.tile([P, G, D], F32, name="o_ps2", tag="s_ps")
+            else:
+                o_ps = ps_out.tile([P, G, D], F32, name="o_ps")
             for i in range(lo, heads if hi is None else hi):
+                tiles["o_ps", u, i] = o_ps
                 nc.tensor.matmul_mx(
-                    out=tiles["o_ps", u][:, i, :],
+                    out=o_ps[:, i, :],
                     lhsT=tiles["e_codes", u][:, i * P : (i + 1) * P].bitcast(FP8X4),
                     lhsT_scale=tiles["e_scales", u][:, i * P : (i + 1) * P],
                     rhs=v_codes[:, kv * D : (kv + 1) * D].bitcast(FP8X4),
@@ -247,12 +250,12 @@ def tile_mistralselfattention_pb_kernel(tc, q_rot, k_rot, v, mask_w, mask_b, out
             for i in range(lo, units[u][3] if hi is None else hi):
                 if eng == "V":
                     nc.vector.tensor_scalar(
-                        out=tiles["o_sb", u][:, i, :], in0=tiles["o_ps", u][:, i, :],
+                        out=tiles["o_sb", u][:, i, :], in0=tiles["o_ps", u, i][:, i, :],
                         scalar1=tiles["recip", u][:, i : i + 1], scalar2=None, op0=ALU.mult,
                     )
                 else:
                     nc.scalar.activation(
-                        out=tiles["o_sb", u][:, i, :], in_=tiles["o_ps", u][:, i, :], func=ACT.Copy,
+                        out=tiles["o_sb", u][:, i, :], in_=tiles["o_ps", u, i][:, i, :], func=ACT.Copy,
                         scale=tiles["recip", u][:, i : i + 1],
                     )
 
@@ -286,7 +289,12 @@ def tile_mistralselfattention_pb_kernel(tc, q_rot, k_rot, v, mask_w, mask_b, out
         add_bias(0, 3, eng="V")
         for k in range(-1, 14):
             run(quantise_e, k - 2)
-            run(scores_matmul, k + 2)
+            run(invert_sums, k - 2)
+            if k + 2 < NG - 1:
+                scores_matmul(k + 2)
+            else:
+                scores_matmul(NG - 1, 2)
+                scores_matmul(NG - 1, 0, 2)
             run(values_matmul, k - 2)
             if 0 < k + 3 < KV:
                 turn_keys(k + 3)
@@ -300,51 +308,63 @@ def tile_mistralselfattention_pb_kernel(tc, q_rot, k_rot, v, mask_w, mask_b, out
                 copy_keys(k + 3)
             run(copy_queries, k + 3)
             run(group_e, k)
-            run(weigh_scores, k + 2)
-            run(add_bias, k + 2)
+            if k + 2 < NG - 1:
+                weigh_scores(k + 2)
+                add_bias(k + 2)
+            else:
+                weigh_scores(NG - 1, 2)
+                weigh_scores(NG - 1, 0, 2)
+                add_bias(NG - 1, 0, 2)
             if k == 0:
                 nc.vector.quantize_mx(
                     out=v_codes[:].bitcast(FP8X4), scales=v_scales[:],
                     in_=v_grouped[:].rearrange("p c t -> p (c t)"),
                 )
-        a, b, c = 14, 15, 16
-        quantise_e(a - 2)
-        scores_matmul(c)
-        values_matmul(a - 2)
-        row_maxima(a, 0, 2)
-        weigh_scores(c)
-        exponentials(a, 0, 2)
-        turn_e(a, 0, 2)
-        normalise(a - 2)
-        store(a - 2)
-        quantise_e(a - 1)
-        add_bias(c)
-        values_matmul(a - 1)
-        group_e(a, 0, 2)
-        row_maxima(a, 2)
-        exponentials(a, 2)
-        turn_e(a, 2)
-        row_maxima(b)
-        exponentials(b)
-        row_maxima(c)
-        exponentials(c)
-        turn_e(b)
-        normalise(a - 1)
-        store(a - 1)
-        turn_e(c, spare=True)
-        group_e(a, 2, eng="V")
-        quantise_e(a)
-        values_matmul(a, spare=True)
-        group_e(b, eng="V")
-        quantise_e(b)
-        values_matmul(b, spare=True)
-        group_e(c)
-        quantise_e(c)
-        values_matmul(c, spare=True)
-        normalise(a)
-        store(a)
-        normalise(b, eng="V")
-        store(b)
-        normalise(c, 0, 1)
-        normalise(c, 1, eng="V")
-        store(c)
+        y, z = NG - 2, NG - 1
+        quantise_e(y - 2)
+        invert_sums(y - 2)
+        values_matmul(y - 2)
+        row_maxima(y)
+        spread_bias(QT - 1)
+        exponentials(y)
+        turn_e(y)
+        normalise(y - 2)
+        store(y - 2)
+        add_bias(z, 2, 3)
+        add_bias(z, 3, eng="V")
+        row_maxima(z, 0, 2)
+        exponentials(z, 0, 2)
+        quantise_e(y - 1)
+        invert_sums(y - 1)
+        values_matmul(y - 1)
+        row_maxima(z, 3)
+        group_e(y, 0, 2, eng="V")
+        turn_e(z, 0, 2)
+        exponentials(z, 3)
+        turn_e(z, 3, spare=True)
+        row_maxima(z, 2, 3)
+        group_e(y, 2, eng="V")
+        normalise(y - 1)
+        store(y - 1)
+        exponentials(z, 2, 3)
+        turn_e(z, 2, 3, spare=True)
+        quantise_e(y)
+        invert_sums(y)
+        values_matmul(y, spare=True)
+        group_e(z, 3)
+        group_e(z, 0, 2, eng="V")
+        quantise_e(z, 0, 2)
+        group_e(z, 2, 3)
+        invert_sums(z)
+        values_matmul(z, 0, 2, spare=True)
+        quantise_e(z, 3)
+        values_matmul(z, 3, spare=True)
+        quantise_e(z, 2, 3)
+        values_matmul(z, 2, 3, spare=True)
+        normalise(y)
+        store(y)
+        normalise(z, 0, 2, eng="V")
+        store(z, 0, 2)
+        normalise(z, 3)
+        normalise(z, 2, 3, eng="V")
+        store(z, 2)

@@ -132,8 +132,8 @@ def tile_mistralselfattention_pb_kernel(tc, q_rot, k_rot, v, mask_w, mask_b, out
                     op0=ALU.mult, op1=ALU.mult,
                 )
 
-        def spread_bias(qt):
-            b_ps = ps_scores.tile([P, T], F32, name="b_ps", tag="s_ps")
+        def spread_bias(qt, pool, tag):
+            b_ps = pool.tile([P, T], F32, name="b_ps", tag=tag)
             nc.tensor.matmul(b_ps[:], lhsT=ident_bf[:], rhs=mb_sb[qt][:], start=True, stop=True)
             tiles["b_ps", qt] = b_ps
 
@@ -231,7 +231,7 @@ def tile_mistralselfattention_pb_kernel(tc, q_rot, k_rot, v, mask_w, mask_b, out
             if spare:
                 o_ps = ps_scores.tile([P, G, D], F32, name="o_ps2", tag="s_ps")
             else:
-                o_ps = ps_out.tile([P, G, D], F32, name="o_ps")
+                o_ps = ps_out.tile([P, G, D], F32, name="o_ps", tag="o_ps")
             for i in range(lo, heads if hi is None else hi):
                 tiles["o_ps", u, i] = o_ps
                 nc.tensor.matmul_mx(
@@ -276,18 +276,24 @@ def tile_mistralselfattention_pb_kernel(tc, q_rot, k_rot, v, mask_w, mask_b, out
         copy_keys(0)
         copy_queries(0, 1, eng="V")
         scores_matmul(0)
-        weigh_scores(0, 0, 1)
-        add_bias(0, 0, 1)
-        spread_bias(0)
         turn_keys(1)
         turn_queries(1)
         copy_keys(1)
         copy_queries(1)
         nc.scalar.copy(out=v_grouped[:], in_=v_sb[:].rearrange("p t c -> p c t"))
-        weigh_scores(0, 1)
+        weigh_scores(0)
+        add_bias(0, 0, 1)
         add_bias(0, 1, 3)
+        scores_matmul(1)
+        spread_bias(0, ps_out, "o_ps")
+        turn_keys(2)
+        turn_queries(2)
+        copy_keys(2)
+        copy_queries(2)
+        weigh_scores(1)
         add_bias(0, 3, eng="V")
-        for k in range(-1, 14):
+        add_bias(1)
+        for k in range(0, 14):
             run(quantise_e, k - 2)
             run(invert_sums, k - 2)
             if k + 2 < NG - 1:
@@ -325,7 +331,7 @@ def tile_mistralselfattention_pb_kernel(tc, q_rot, k_rot, v, mask_w, mask_b, out
         invert_sums(y - 2)
         values_matmul(y - 2)
         row_maxima(y)
-        spread_bias(QT - 1)
+        spread_bias(QT - 1, ps_scores, "s_ps")
         exponentials(y)
         turn_e(y)
         normalise(y - 2)

@@ -259,25 +259,26 @@ def tile_mistralselfattention_pb_kernel(tc, q_rot, k_rot, v, mask_w, mask_b, out
                         scale=tiles["recip", u][:, i : i + 1],
                     )
 
-        def store(u, lo=0, hi=None):
+        def store(u, lo=0, hi=None, queue=nc.sync):
             qt, kv, first, heads = units[u]
             hi = heads if hi is None else hi
             h0 = kv * G + first
-            nc.sync.dma_start(out=out_view[:, qt, h0 + lo : h0 + hi, :], in_=tiles["o_sb", u][:, lo:hi])
+            queue.dma_start(out=out_view[:, qt, h0 + lo : h0 + hi, :], in_=tiles["o_sb", u][:, lo:hi])
 
         def run(stage, u, *more, **kw):
             if 0 <= u < n_units:
                 stage(u, *more, **kw)
 
-        turn_queries(0, 0, 1)
         turn_keys(0)
-        turn_queries(0, 1)
+        turn_queries(0)
         copy_queries(0, 0, 1, eng="V")
         copy_keys(0)
         copy_queries(0, 1, eng="V")
-        scores_matmul(0)
+        scores_matmul(0, 0, 2)
         turn_keys(1)
+        scores_matmul(0, 2, 3)
         turn_queries(1)
+        scores_matmul(0, 3)
         copy_keys(1)
         copy_queries(1)
         nc.scalar.copy(out=v_grouped[:], in_=v_sb[:].rearrange("p t c -> p c t"))
@@ -372,5 +373,6 @@ def tile_mistralselfattention_pb_kernel(tc, q_rot, k_rot, v, mask_w, mask_b, out
         normalise(z, 0, 2, eng="V")
         store(z, 0, 2)
         normalise(z, 3)
+        store(z, 3, queue=nc.scalar)
         normalise(z, 2, 3, eng="V")
-        store(z, 2)
+        store(z, 2, 3)

@@ -24,6 +24,7 @@ PACK = 4
 HALF = T // 2
 NG = QT * KV
 PAIRED = 14
+TURNED = range(5, 12)
 SCALE = 1.0 / math.sqrt(D)
 
 FLOPS = 2 * 2 * H * T * T * D
@@ -87,6 +88,21 @@ def tile_mistralselfattention_pb_kernel(tc, q_rot, k_rot, v, mask_w, mask_b, out
         v_codes = keep.tile([P, KV * D], U32, align_bytes=64)
         v_scales = keep.tile([P, KV * D], U8, align_bytes=64)
 
+        wT = {}
+        bT = {}
+
+        def turn_mask(qt, which):
+            m_ps = ps_out.tile([P, QT, P], BF16, name="m_ps", tag="o_ps")
+            source = (mw_sb, mb_sb)[which][qt]
+            for kt in range(QT):
+                nc.tensor.transpose(m_ps[:, kt, :], source[:, kt * P : (kt + 1) * P], ident_bf[:])
+            if which == 0:
+                wT[qt] = keep.tile([P, QT, P], BF16, name="wT%d" % qt)
+                nc.scalar.copy(out=wT[qt][:], in_=m_ps[:])
+            else:
+                bT[qt] = keep.tile([P, QT, P], F32, name="bT%d" % qt)
+                nc.scalar.copy(out=bT[qt][:], in_=m_ps[:])
+
         tiles = {}
 
         def turn_keys(kv):
@@ -117,9 +133,16 @@ def tile_mistralselfattention_pb_kernel(tc, q_rot, k_rot, v, mask_w, mask_b, out
             qt, kv, first, heads = units[u]
             for i in range(lo, heads if hi is None else hi):
                 s_ps = ps_scores.tile([P, T], F32, tag="s_ps")
-                nc.tensor.matmul(
-                    s_ps[:], lhsT=tiles["qT", u][:, i, :], rhs=kT[:, kv, :], start=True, stop=True
-                )
+                if u in TURNED and i == G - 1:
+                    for kt in range(QT):
+                        keys = slice(kt * P, (kt + 1) * P)
+                        nc.tensor.matmul(
+                            s_ps[:, keys], lhsT=kT[:, kv, keys], rhs=tiles["qT", u][:, i, :], start=True, stop=True
+                        )
+                else:
+                    nc.tensor.matmul(
+                        s_ps[:], lhsT=tiles["qT", u][:, i, :], rhs=kT[:, kv, :], start=True, stop=True
+                    )
                 tiles["s_ps", u, i] = s_ps
 
         def weigh_scores(u, lo=0, hi=None):
@@ -127,10 +150,38 @@ def tile_mistralselfattention_pb_kernel(tc, q_rot, k_rot, v, mask_w, mask_b, out
             if ("s2", u) not in tiles:
                 tiles["s2", u] = work.tile([P, G, T], F32, bufs=4, name="s2")
             for i in range(lo, heads if hi is None else hi):
+                weight = mw_sb[qt][:]
+                if u in TURNED and i == G - 1:
+                    weight = wT[qt][:].rearrange("p kt q -> p (kt q)")
                 nc.vector.scalar_tensor_tensor(
-                    out=tiles["s2", u][:, i, :], in0=tiles["s_ps", u, i][:], scalar=SCALE, in1=mw_sb[qt][:],
+                    out=tiles["s2", u][:, i, :], in0=tiles["s_ps", u, i][:], scalar=SCALE, in1=weight,
                     op0=ALU.mult, op1=ALU.mult,
                 )
+
+        def take_scores(u):
+            nc.scalar.activation(
+                out=tiles["s2", u][:, G - 1, :], in_=tiles["s_ps", u, G - 1][:], func=ACT.Copy, scale=SCALE
+            )
+
+        def weigh_taken(u):
+            p = tiles["s2", u][:, G - 1, :]
+            nc.gpsimd.tensor_tensor(
+                out=p, in0=p, in1=wT[units[u][0]][:].rearrange("p kt q -> p (kt q)"), op=ALU.mult
+            )
+
+        def turn_back(u):
+            qt = units[u][0]
+            t_ps = ps_scores.tile([P, T], F32, name="t_ps", tag="s_ps")
+            for kt in range(QT):
+                keys = slice(kt * P, (kt + 1) * P)
+                nc.tensor.matmul(
+                    t_ps[:, keys], lhsT=bT[qt][:, kt, :], rhs=ident_f32[:], is_transpose=True, start=True, stop=False
+                )
+                nc.tensor.matmul(
+                    t_ps[:, keys], lhsT=tiles["s2", u][:, G - 1, keys], rhs=ident_f32[:], is_transpose=True,
+                    start=False, stop=True,
+                )
+            tiles["t_ps", u] = t_ps
 
         def spread_bias(qt, pool, tag):
             b_ps = pool.tile([P, T], F32, name="b_ps", tag=tag)
@@ -155,9 +206,11 @@ def tile_mistralselfattention_pb_kernel(tc, q_rot, k_rot, v, mask_w, mask_b, out
             if lo == 0:
                 tiles["neg_max", u] = work.tile([P, G], F32, name="neg_max")
             for i in range(lo, units[u][3] if hi is None else hi, step):
+                source = tiles["s2", u][:, i : i + step, :]
+                if u in TURNED and i == G - 1:
+                    source = tiles["t_ps", u][:]
                 nc.vector.tensor_reduce(
-                    out=tiles["neg_max", u][:, i : i + step], in_=tiles["s2", u][:, i : i + step, :], axis=AXIS.X,
-                    op=ALU.max, negate=True,
+                    out=tiles["neg_max", u][:, i : i + step], in_=source, axis=AXIS.X, op=ALU.max, negate=True
                 )
 
         def exponentials(u, lo=0, hi=None):
@@ -169,8 +222,9 @@ def tile_mistralselfattention_pb_kernel(tc, q_rot, k_rot, v, mask_w, mask_b, out
                 if u >= PAIRED or u % 2 == 0:
                     tiles["rowsums", u] = sums
             for i in range(lo, units[u][3] if hi is None else hi):
+                source = tiles["t_ps", u][:] if u in TURNED and i == G - 1 else tiles["s2", u][:, i, :]
                 nc.scalar.activation(
-                    out=tiles["e_sb", u][:, i, :], in_=tiles["s2", u][:, i, :], func=ACT.Exp,
+                    out=tiles["e_sb", u][:, i, :], in_=source, func=ACT.Exp,
                     bias=tiles["neg_max", u][:, i : i + 1], scale=1.0,
                     accum_out=tiles["rowsum", u][:, i : i + 1],
                 )
@@ -274,11 +328,9 @@ def tile_mistralselfattention_pb_kernel(tc, q_rot, k_rot, v, mask_w, mask_b, out
         copy_queries(0, 0, 1, eng="V")
         copy_keys(0)
         copy_queries(0, 1, eng="V")
-        scores_matmul(0, 0, 2)
+        scores_matmul(0)
         turn_keys(1)
-        scores_matmul(0, 2, 3)
         turn_queries(1)
-        scores_matmul(0, 3)
         copy_keys(1)
         copy_queries(1)
         nc.scalar.copy(out=v_grouped[:], in_=v_sb[:].rearrange("p t c -> p c t"))
@@ -294,34 +346,62 @@ def tile_mistralselfattention_pb_kernel(tc, q_rot, k_rot, v, mask_w, mask_b, out
         weigh_scores(1)
         add_bias(0, 3, eng="V")
         add_bias(1)
-        for k in range(0, 14):
+        for k in range(14):
+            ahead = k + 2
+            turned = k in TURNED
+            lead = ahead in TURNED
+            by_scalar = lead and ahead % 2 == 0
             run(quantise_e, k - 2)
             run(invert_sums, k - 2)
-            if k + 2 < NG - 1:
-                scores_matmul(k + 2)
+            if k < 4:
+                turn_mask(1 + k // 2, k % 2)
+            row_maxima(k, 0, 2, step=2)
+            if turned:
+                row_maxima(k, 2, 3)
             else:
-                scores_matmul(NG - 1, 2)
-                scores_matmul(NG - 1, 0, 2)
-            run(values_matmul, k - 2)
-            if 0 < k + 3 < KV:
+                row_maxima(k, 2, 4, step=2)
+            if k + 3 < KV:
                 turn_keys(k + 3)
+            if ahead == NG - 1:
+                heads = (2, 3, 0, 1)
+            elif lead and not by_scalar:
+                heads = (3, 0, 1, 2)
+            else:
+                heads = (0, 1, 2, 3)
+            products = [i for i in heads if not (by_scalar and i == G - 1)]
+            for i in heads[:2]:
+                scores_matmul(ahead, i, i + 1)
+            if turned:
+                turn_back(k)
+            scores_matmul(ahead, heads[2], heads[2] + 1)
+            for i in products[:2]:
+                weigh_scores(ahead, i, i + 1)
+            scores_matmul(ahead, heads[3], heads[3] + 1)
+            if turned:
+                row_maxima(k, 3)
+            for i in products[2:]:
+                weigh_scores(ahead, i, i + 1)
+            run(values_matmul, k - 2)
             run(turn_queries, k + 3)
-            run(row_maxima, k, step=2)
-            run(exponentials, k)
-            run(turn_e, k)
-            run(normalise, k - 2)
-            run(store, k - 2)
-            if 0 < k + 3 < KV:
+            exponentials(k)
+            turn_e(k)
+            if k + 3 < KV:
                 copy_keys(k + 3)
             run(copy_queries, k + 3)
-            run(group_e, k)
-            if k + 2 < NG - 1:
-                weigh_scores(k + 2)
-                add_bias(k + 2)
+            if by_scalar:
+                take_scores(ahead)
+            group_e(k, 0, 2)
+            run(normalise, k - 2)
+            run(store, k - 2)
+            group_e(k, 2)
+            if ahead == NG - 1:
+                add_bias(ahead, 0, 2)
+            elif lead:
+                add_bias(ahead, 0, 3)
             else:
-                weigh_scores(NG - 1, 2)
-                weigh_scores(NG - 1, 0, 2)
-                add_bias(NG - 1, 0, 2)
+                add_bias(ahead)
+            if by_scalar:
+                weigh_taken(ahead)
             if k == 0:
                 nc.vector.quantize_mx(
                     out=v_codes[:].bitcast(FP8X4), scales=v_scales[:],

@@ -24,7 +24,7 @@ PACK = 4
 HALF = T // 2
 NG = QT * KV
 PAIRED = 14
-TURNED = range(5, 12)
+TURNED = range(4, 14)
 SCALE = 1.0 / math.sqrt(D)
 
 FLOPS = 2 * 2 * H * T * T * D
@@ -62,9 +62,10 @@ def tile_mistralselfattention_pb_kernel(tc, q_rot, k_rot, v, mask_w, mask_b, out
             if qt == 0:
                 nc.sync.dma_start(out=k_sb[kv][:], in_=k_view[:, :, kv, :])
             nc.sync.dma_start(out=q_sb[g][:], in_=q_view[:, qt, kv * G : (kv + 1) * G, :])
-            if kv == 0:
-                nc.sync.dma_start(out=mw_sb[qt][:], in_=mw_view[:, qt])
-                nc.sync.dma_start(out=mb_sb[qt][:], in_=mb_view[:, qt])
+            if g == 0 or g == KV - 1:
+                for j in range(min(g, 1), 1 if g == 0 else QT):
+                    nc.sync.dma_start(out=mw_sb[j][:], in_=mw_view[:, j])
+                    nc.sync.dma_start(out=mb_sb[j][:], in_=mb_view[:, j])
             if g == 1:
                 nc.sync.dma_start(out=v_sb[:], in_=v_view)
 
@@ -91,8 +92,8 @@ def tile_mistralselfattention_pb_kernel(tc, q_rot, k_rot, v, mask_w, mask_b, out
         wT = {}
         bT = {}
 
-        def turn_mask(qt, which):
-            m_ps = ps_out.tile([P, QT, P], BF16, name="m_ps", tag="o_ps")
+        def turn_mask(qt, which, pool, tag):
+            m_ps = pool.tile([P, QT, P], BF16, name="m_ps", tag=tag)
             source = (mw_sb, mb_sb)[which][qt]
             for kt in range(QT):
                 nc.tensor.transpose(m_ps[:, kt, :], source[:, kt * P : (kt + 1) * P], ident_bf[:])
@@ -117,7 +118,7 @@ def tile_mistralselfattention_pb_kernel(tc, q_rot, k_rot, v, mask_w, mask_b, out
         def turn_queries(u, lo=0, hi=None):
             qt, kv, first, heads = units[u]
             if lo == 0:
-                tiles["qT_ps", u] = ps_q.tile([P, G, P], BF16, name="qT_ps")
+                tiles["qT_ps", u] = ps_q.tile([P, G, P], BF16, name="qT_ps", tag="qT_ps")
                 tiles["qT", u] = work.tile([P, G, P], BF16, name="qT")
             for i in range(lo, heads if hi is None else hi):
                 nc.tensor.transpose(tiles["qT_ps", u][:, i, :], q_sb[qt * KV + kv][:, first + i, :], ident_bf[:])
@@ -350,11 +351,13 @@ def tile_mistralselfattention_pb_kernel(tc, q_rot, k_rot, v, mask_w, mask_b, out
             ahead = k + 2
             turned = k in TURNED
             lead = ahead in TURNED
-            by_scalar = lead and ahead % 2 == 0
+            by_scalar = lead and ahead % 2 == 1
             run(quantise_e, k - 2)
             run(invert_sums, k - 2)
             if k < 4:
-                turn_mask(1 + k // 2, k % 2)
+                turn_mask(1 + k // 2, k % 2, ps_out, "o_ps")
+            if 2 <= k < 4:
+                turn_mask(3, k - 2, ps_q, "qT_ps")
             row_maxima(k, 0, 2, step=2)
             if turned:
                 row_maxima(k, 2, 3)

@@ -24,7 +24,8 @@ PACK = 4
 HALF = T // 2
 NG = QT * KV
 PAIRED = 14
-TURNED = range(4, 14)
+TURNED = tuple(range(4, 14)) + (15,)
+TAKEN = 384
 SCALE = 1.0 / math.sqrt(D)
 
 FLOPS = 2 * 2 * H * T * T * D
@@ -159,15 +160,21 @@ def tile_mistralselfattention_pb_kernel(tc, q_rot, k_rot, v, mask_w, mask_b, out
                     op0=ALU.mult, op1=ALU.mult,
                 )
 
+        def weigh_part(u):
+            nc.vector.scalar_tensor_tensor(
+                out=tiles["s2", u][:, G - 1, TAKEN:], in0=tiles["s_ps", u, G - 1][:, TAKEN:], scalar=SCALE,
+                in1=wT[units[u][0]][:].rearrange("p kt q -> p (kt q)")[:, TAKEN:], op0=ALU.mult, op1=ALU.mult,
+            )
+
         def take_scores(u):
             nc.scalar.activation(
-                out=tiles["s2", u][:, G - 1, :], in_=tiles["s_ps", u, G - 1][:], func=ACT.Copy, scale=SCALE
+                out=tiles["s2", u][:, G - 1, :TAKEN], in_=tiles["s_ps", u, G - 1][:, :TAKEN], func=ACT.Copy, scale=SCALE
             )
 
         def weigh_taken(u):
-            p = tiles["s2", u][:, G - 1, :]
+            p = tiles["s2", u][:, G - 1, :TAKEN]
             nc.gpsimd.tensor_tensor(
-                out=p, in0=p, in1=wT[units[u][0]][:].rearrange("p kt q -> p (kt q)"), op=ALU.mult
+                out=p, in0=p, in1=wT[units[u][0]][:].rearrange("p kt q -> p (kt q)")[:, :TAKEN], op=ALU.mult
             )
 
         def turn_back(u):
@@ -351,7 +358,7 @@ def tile_mistralselfattention_pb_kernel(tc, q_rot, k_rot, v, mask_w, mask_b, out
             ahead = k + 2
             turned = k in TURNED
             lead = ahead in TURNED
-            by_scalar = lead and ahead % 2 == 1
+            by_scalar = lead and ahead % 2 == 1 and ahead < 15
             run(quantise_e, k - 2)
             run(invert_sums, k - 2)
             if k < 4:
@@ -382,6 +389,8 @@ def tile_mistralselfattention_pb_kernel(tc, q_rot, k_rot, v, mask_w, mask_b, out
             scores_matmul(ahead, heads[3], heads[3] + 1)
             if turned:
                 row_maxima(k, 3)
+            if by_scalar:
+                weigh_part(ahead)
             for i in products[2:]:
                 weigh_scores(ahead, i, i + 1)
             run(values_matmul, k - 2)
@@ -393,10 +402,9 @@ def tile_mistralselfattention_pb_kernel(tc, q_rot, k_rot, v, mask_w, mask_b, out
             run(copy_queries, k + 3)
             if by_scalar:
                 take_scores(ahead)
-            group_e(k, 0, 2)
             run(normalise, k - 2)
             run(store, k - 2)
-            group_e(k, 2)
+            group_e(k)
             if ahead == NG - 1:
                 add_bias(ahead, 0, 2)
             elif lead:
@@ -414,14 +422,13 @@ def tile_mistralselfattention_pb_kernel(tc, q_rot, k_rot, v, mask_w, mask_b, out
         quantise_e(y - 2)
         invert_sums(y - 2)
         values_matmul(y - 2)
+        turn_back(z)
         row_maxima(y)
-        spread_bias(QT - 1, ps_scores, "s_ps")
         exponentials(y)
         turn_e(y)
         normalise(y - 2)
         store(y - 2)
         add_bias(z, 2, 3)
-        add_bias(z, 3, eng="V")
         row_maxima(z, 0, 2)
         exponentials(z, 0, 2)
         quantise_e(y - 1)

from contextlib import ExitStack
import math

import concourse.mybir as mybir
from concourse.masks import make_identity

BF16 = mybir.dt.bfloat16
F32 = mybir.dt.float32
U32 = mybir.dt.uint32
U8 = mybir.dt.uint8
FP8X4 = mybir.dt.float8_e4m3fn_x4
ALU = mybir.AluOpType
ACT = mybir.ActivationFunctionType
AXIS = mybir.AxisListType

P = 128
T = 512
H = 16
KV = 4
D = 128
G = H // KV
QT = T // P
PACK = 4
HALF = T // 2
NG = QT * KV
PAIRED = 14
TURNED = tuple(range(4, 14)) + (15,)
TAKEN = 384
SCALE = 1.0 / math.sqrt(D)

FLOPS = 2 * 2 * H * T * T * D


def tile_mistralselfattention_pb_kernel(tc, q_rot, k_rot, v, mask_w, mask_b, out):
    nc = tc.nc

    q_view = q_rot.rearrange("b (qt p) h d -> p (b qt) h d", p=P)
    k_view = k_rot.rearrange("b (kt p) kv d -> p (b kt) kv d", p=P)
    mw_view = mask_w.rearrange("a b (qt p) k -> p (a b qt) k", p=P)
    mb_view = mask_b.rearrange("a b (qt p) k -> p (a b qt) k", p=P)
    out_view = out.rearrange("b (qt p) h d -> p (b qt) h d", p=P)
    v_view = v.rearrange("b (p t) kv d -> p (b t) (kv d)", t=PACK)

    units = [(g // KV, g % KV, 0, G) for g in range(NG)]
    n_units = NG

    with ExitStack() as ctx:
        keep = ctx.enter_context(tc.tile_pool(name="keep", bufs=1))
        work = ctx.enter_context(tc.tile_pool(name="work", bufs=3))
        ps_scores = ctx.enter_context(tc.psum_pool(name="ps_scores", bufs=G))
        ps_e = ctx.enter_context(tc.psum_pool(name="ps_e", bufs=2))
        ps_q = ctx.enter_context(tc.psum_pool(name="ps_q", bufs=1))
        ps_out = ctx.enter_context(tc.psum_pool(name="ps_out", bufs=1))
        ctx.enter_context(tc.manual_schedule())

        k_sb = [keep.tile([P, QT, D], BF16, name="k_sb%d" % kv) for kv in range(KV)]
        q_sb = [keep.tile([P, G, D], BF16, name="q_sb%d" % g) for g in range(NG)]
        mw_sb = [keep.tile([P, T], BF16, name="mw_sb%d" % qt) for qt in range(QT)]
        mb_sb = [keep.tile([P, T], BF16, name="mb_sb%d" % qt) for qt in range(QT)]
        v_sb = keep.tile([P, PACK, KV * D], BF16)
        for g in range(NG):
            qt, kv = divmod(g, KV)
            if qt == 0:
                nc.sync.dma_start(out=k_sb[kv][:], in_=k_view[:, :, kv, :])
            nc.sync.dma_start(out=q_sb[g][:], in_=q_view[:, qt, kv * G : (kv + 1) * G, :])
            if g == 0 or g == KV - 1:
                for j in range(min(g, 1), 1 if g == 0 else QT):
                    nc.sync.dma_start(out=mw_sb[j][:], in_=mw_view[:, j])
                    nc.sync.dma_start(out=mb_sb[j][:], in_=mb_view[:, j])
            if g == 1:
                nc.sync.dma_start(out=v_sb[:], in_=v_view)

        zeros = keep.tile([P, P], BF16)
        nc.vector.memset(zeros[:], 0.0)
        for i in range(4):
            dummy = ps_scores.tile([P, 4, P], F32, tag="s_ps")
            nc.tensor.matmul(
                dummy[:], lhsT=zeros[:], rhs=zeros[:].unsqueeze(1).to_broadcast([P, 4, P]), start=True, stop=True
            )
        ident_bf = keep.tile([P, P], BF16)
        make_identity(nc, ident_bf[:])
        ident_f32 = keep.tile([P, P], F32)
        make_identity(nc, ident_f32[:])
        warm = keep.tile([P, 1], F32)
        nc.vector.memset(warm[:], 0.0)
        nc.scalar.activation(out=warm[:], in_=warm[:], func=ACT.Exp)

        kT = keep.tile([P, KV, T], BF16)
        v_grouped = keep.tile([P, KV * D, PACK], BF16, align_bytes=64)
        v_codes = keep.tile([P, KV * D], U32, align_bytes=64)
        v_scales = keep.tile([P, KV * D], U8, align_bytes=64)

        wT = {}
        bT = {}

        def turn_mask(qt, which, pool, tag):
            m_ps = pool.tile([P, QT, P], BF16, name="m_ps", tag=tag)
            source = (mw_sb, mb_sb)[which][qt]
            for kt in range(QT):
                nc.tensor.transpose(m_ps[:, kt, :], source[:, kt * P : (kt + 1) * P], ident_bf[:])
            if which == 0:
                wT[qt] = keep.tile([P, QT, P], BF16, name="wT%d" % qt)
                nc.scalar.copy(out=wT[qt][:], in_=m_ps[:])
            else:
                bT[qt] = keep.tile([P, QT, P], F32, name="bT%d" % qt)
                nc.scalar.copy(out=bT[qt][:], in_=m_ps[:])

        tiles = {}

        def turn_keys(kv):
            kT_ps = ps_e.tile([P, QT, P], BF16, tag="eT_ps")
            for kt in range(QT):
                nc.tensor.transpose(kT_ps[:, kt, :], k_sb[kv][:, kt, :], ident_bf[:])
            tiles["kT_ps", kv] = kT_ps

        def copy_keys(kv):
            nc.scalar.copy(out=kT[:, kv, :], in_=tiles["kT_ps", kv][:].rearrange("d kt p -> d (kt p)"))

        def turn_queries(u, lo=0, hi=None):
            qt, kv, first, heads = units[u]
            if lo == 0:
                tiles["qT_ps", u] = ps_q.tile([P, G, P], BF16, name="qT_ps", tag="qT_ps")
                tiles["qT", u] = work.tile([P, G, P], BF16, name="qT")
            for i in range(lo, heads if hi is None else hi):
                nc.tensor.transpose(tiles["qT_ps", u][:, i, :], q_sb[qt * KV + kv][:, first + i, :], ident_bf[:])

        def copy_queries(u, lo=0, hi=None, eng=None):
            hi = units[u][3] if hi is None else hi
            if eng == "V":
                nc.vector.tensor_copy(out=tiles["qT", u][:, lo:hi], in_=tiles["qT_ps", u][:, lo:hi])
            else:
                nc.scalar.copy(out=tiles["qT", u][:, lo:hi], in_=tiles["qT_ps", u][:, lo:hi])

        def scores_matmul(u, lo=0, hi=None):
            qt, kv, first, heads = units[u]
            for i in range(lo, heads if hi is None else hi):
                s_ps = ps_scores.tile([P, T], F32, tag="s_ps")
                if u in TURNED and i == G - 1:
                    for kt in range(QT):
                        keys = slice(kt * P, (kt + 1) * P)
                        nc.tensor.matmul(
                            s_ps[:, keys], lhsT=kT[:, kv, keys], rhs=tiles["qT", u][:, i, :], start=True, stop=True
                        )
                else:
                    nc.tensor.matmul(
                        s_ps[:], lhsT=tiles["qT", u][:, i, :], rhs=kT[:, kv, :], start=True, stop=True
                    )
                tiles["s_ps", u, i] = s_ps

        def weigh_scores(u, lo=0, hi=None):
            qt, kv, first, heads = units[u]
            if ("s2", u) not in tiles:
                tiles["s2", u] = work.tile([P, G, T], F32, bufs=4, name="s2")
            for i in range(lo, heads if hi is None else hi):
                weight = mw_sb[qt][:]
                if u in TURNED and i == G - 1:
                    weight = wT[qt][:].rearrange("p kt q -> p (kt q)")
                nc.vector.scalar_tensor_tensor(
                    out=tiles["s2", u][:, i, :], in0=tiles["s_ps", u, i][:], scalar=SCALE, in1=weight,
                    op0=ALU.mult, op1=ALU.mult,
                )

        def weigh_part(u):
            nc.vector.scalar_tensor_tensor(
                out=tiles["s2", u][:, G - 1, TAKEN:], in0=tiles["s_ps", u, G - 1][:, TAKEN:], scalar=SCALE,
                in1=wT[units[u][0]][:].rearrange("p kt q -> p (kt q)")[:, TAKEN:], op0=ALU.mult, op1=ALU.mult,
            )

        def take_scores(u):
            nc.scalar.activation(
                out=tiles["s2", u][:, G - 1, :TAKEN], in_=tiles["s_ps", u, G - 1][:, :TAKEN], func=ACT.Copy, scale=SCALE
            )

        def weigh_taken(u):
            p = tiles["s2", u][:, G - 1, :TAKEN]
            nc.gpsimd.tensor_tensor(
                out=p, in0=p, in1=wT[units[u][0]][:].rearrange("p kt q -> p (kt q)")[:, :TAKEN], op=ALU.mult
            )

        def turn_back(u):
            qt = units[u][0]
            t_ps = ps_scores.tile([P, T], F32, name="t_ps", tag="s_ps")
            for kt in range(QT):
                keys = slice(kt * P, (kt + 1) * P)
                nc.tensor.matmul(
                    t_ps[:, keys], lhsT=bT[qt][:, kt, :], rhs=ident_f32[:], is_transpose=True, start=True, stop=False
                )
                nc.tensor.matmul(
                    t_ps[:, keys], lhsT=tiles["s2", u][:, G - 1, keys], rhs=ident_f32[:], is_transpose=True,
                    start=False, stop=True,
                )
            tiles["t_ps", u] = t_ps

        def spread_bias(qt, pool, tag):
            b_ps = pool.tile([P, T], F32, name="b_ps", tag=tag)
            nc.tensor.matmul(b_ps[:], lhsT=ident_bf[:], rhs=mb_sb[qt][:], start=True, stop=True)
            tiles["b_ps", qt] = b_ps

        def add_bias(u, lo=0, hi=None, eng=None):
            qt, kv, first, heads = units[u]
            hi = heads if hi is None else hi
            s2 = tiles["s2", u][:, lo:hi]
            if eng == "V":
                for i in range(lo, hi):
                    nc.vector.tensor_tensor(
                        out=tiles["s2", u][:, i, :], in0=tiles["s2", u][:, i, :], in1=tiles["b_ps", qt][:], op=ALU.add
                    )
            else:
                nc.gpsimd.tensor_tensor(
                    out=s2, in0=s2, in1=mb_sb[qt][:].unsqueeze(1).to_broadcast([P, hi - lo, T]), op=ALU.add
                )

        def row_maxima(u, lo=0, hi=None, step=1):
            if lo == 0:
                tiles["neg_max", u] = work.tile([P, G], F32, name="neg_max")
            for i in range(lo, units[u][3] if hi is None else hi, step):
                source = tiles["s2", u][:, i : i + step, :]
                if u in TURNED and i == G - 1:
                    source = tiles["t_ps", u][:]
                nc.vector.tensor_reduce(
                    out=tiles["neg_max", u][:, i : i + step], in_=source, axis=AXIS.X, op=ALU.max, negate=True
                )

        def exponentials(u, lo=0, hi=None):
            if lo == 0:
                tiles["e_sb", u] = work.tile([P, G, T], BF16, name="e_sb")
                if u >= PAIRED or u % 2 == 0:
                    sums = work.tile([P, 2, G], F32, bufs=4, name="rowsum")
                tiles["rowsum", u] = sums[:, 0] if u >= PAIRED or u % 2 == 0 else tiles["rowsums", u - 1][:, 1]
                if u >= PAIRED or u % 2 == 0:
                    tiles["rowsums", u] = sums
            for i in range(lo, units[u][3] if hi is None else hi):
                source = tiles["t_ps", u][:] if u in TURNED and i == G - 1 else tiles["s2", u][:, i, :]
                nc.scalar.activation(
                    out=tiles["e_sb", u][:, i, :], in_=source, func=ACT.Exp,
                    bias=tiles["neg_max", u][:, i : i + 1], scale=1.0,
                    accum_out=tiles["rowsum", u][:, i : i + 1],
                )

        def turn_e(u, lo=0, hi=None, spare=False):
            hi = units[u][3] if hi is None else hi
            for first in range(lo, hi, 2):
                if spare:
                    eT_ps = ps_scores.tile([P, 2, 2, P], F32, name="eT_ps2", tag="s_ps")
                else:
                    eT_ps = ps_e.tile([P, 2, 2, P], F32, tag="eT_ps")
                for j in range(min(2, hi - first)):
                    e_words = tiles["e_sb", u][:, first + j, :].bitcast(F32)
                    for half in range(2):
                        nc.tensor.transpose(eT_ps[:, j, half, :], e_words[:, half::2], ident_f32[:])
                tiles["eT_ps", u, first] = eT_ps

        def group_e(u, lo=0, hi=None, eng=None):
            if ("e_grouped", u) not in tiles:
                tiles["e_grouped", u] = work.tile([P, G, P, PACK], BF16, align_bytes=64, name="e_grouped")
            hi = units[u][3] if hi is None else hi
            for first in range(lo, hi, 2):
                w = min(2, hi - first)
                args = dict(
                    out=tiles["e_grouped", u][:, first : first + w].bitcast(F32),
                    in_=tiles["eT_ps", u, first][:, :w].rearrange("p j half q -> p j q half"),
                )
                if eng == "V":
                    nc.vector.tensor_copy(**args)
                else:
                    nc.scalar.copy(**args)

        def quantise_e(u, lo=0, hi=None):
            hi = units[u][3] if hi is None else hi
            if lo == 0:
                tiles["e_codes", u] = work.tile([P, G * P], U32, align_bytes=64, name="e_codes")
                tiles["e_scales", u] = work.tile([P, G * P], U8, align_bytes=64, name="e_scales")
                if u >= PAIRED or u % 2 == 0:
                    inverse = work.tile([P, 2, G], F32, name="recip")
                    tiles["inverse", u] = inverse
                    tiles["recip", u] = inverse[:, 0]
                else:
                    tiles["recip", u] = tiles["inverse", u - 1][:, 1]
            nc.vector.quantize_mx(
                out=tiles["e_codes", u][:, lo * P : hi * P].bitcast(FP8X4),
                scales=tiles["e_scales", u][:, lo * P : hi * P],
                in_=tiles["e_grouped", u][:, lo:hi].rearrange("p i q t -> p (i q t)"),
            )

        def invert_sums(u):
            if u >= PAIRED:
                nc.vector.reciprocal(out=tiles["recip", u], in_=tiles["rowsum", u])
            elif u % 2 == 0:
                nc.vector.reciprocal(out=tiles["inverse", u][:], in_=tiles["rowsums", u][:])

        def values_matmul(u, lo=0, hi=None, spare=False):
            qt, kv, first, heads = units[u]
            if spare:
                o_ps = ps_scores.tile([P, G, D], F32, name="o_ps2", tag="s_ps")
            else:
                o_ps = ps_out.tile([P, G, D], F32, name="o_ps", tag="o_ps")
            for i in range(lo, heads if hi is None else hi):
                tiles["o_ps", u, i] = o_ps
                nc.tensor.matmul_mx(
                    out=o_ps[:, i, :],
                    lhsT=tiles["e_codes", u][:, i * P : (i + 1) * P].bitcast(FP8X4),
                    lhsT_scale=tiles["e_scales", u][:, i * P : (i + 1) * P],
                    rhs=v_codes[:, kv * D : (kv + 1) * D].bitcast(FP8X4),
                    rhs_scale=v_scales[:, kv * D : (kv + 1) * D],
                    start=True,
                    stop=True,
                )

        def normalise(u, lo=0, hi=None, eng=None):
            if lo == 0:
                tiles["o_sb", u] = work.tile([P, G, D], F32, name="o_sb", bufs=5)
            for i in range(lo, units[u][3] if hi is None else hi):
                if eng == "V":
                    nc.vector.tensor_scalar(
                        out=tiles["o_sb", u][:, i, :], in0=tiles["o_ps", u, i][:, i, :],
                        scalar1=tiles["recip", u][:, i : i + 1], scalar2=None, op0=ALU.mult,
                    )
                else:
                    nc.scalar.activation(
                        out=tiles["o_sb", u][:, i, :], in_=tiles["o_ps", u, i][:, i, :], func=ACT.Copy,
                        scale=tiles["recip", u][:, i : i + 1],
                    )

        def store(u, lo=0, hi=None, queue=nc.sync):
            qt, kv, first, heads = units[u]
            hi = heads if hi is None else hi
            h0 = kv * G + first
            queue.dma_start(out=out_view[:, qt, h0 + lo : h0 + hi, :], in_=tiles["o_sb", u][:, lo:hi])

        def run(stage, u, *more, **kw):
            if 0 <= u < n_units:
                stage(u, *more, **kw)

        turn_keys(0)
        turn_queries(0)
        copy_queries(0, 0, 1, eng="V")
        copy_keys(0)
        copy_queries(0, 1, eng="V")
        scores_matmul(0)
        turn_keys(1)
        turn_queries(1)
        copy_keys(1)
        copy_queries(1)
        nc.scalar.copy(out=v_grouped[:], in_=v_sb[:].rearrange("p t c -> p c t"))
        weigh_scores(0)
        add_bias(0, 0, 1)
        add_bias(0, 1, 3)
        scores_matmul(1)
        spread_bias(0, ps_out, "o_ps")
        turn_keys(2)
        turn_queries(2)
        copy_keys(2)
        copy_queries(2)
        weigh_scores(1)
        add_bias(0, 3, eng="V")
        add_bias(1)
        for k in range(14):
            ahead = k + 2
            turned = k in TURNED
            lead = ahead in TURNED
            by_scalar = lead and ahead % 2 == 1 and ahead < 15
            run(quantise_e, k - 2)
            run(invert_sums, k - 2)
            if k < 4:
                turn_mask(1 + k // 2, k % 2, ps_out, "o_ps")
            if 2 <= k < 4:
                turn_mask(3, k - 2, ps_q, "qT_ps")
            row_maxima(k, 0, 2, step=2)
            if turned:
                row_maxima(k, 2, 3)
            else:
                row_maxima(k, 2, 4, step=2)
            if k + 3 < KV:
                turn_keys(k + 3)
            if ahead == NG - 1:
                heads = (2, 3, 0, 1)
            elif lead and not by_scalar:
                heads = (3, 0, 1, 2)
            else:
                heads = (0, 1, 2, 3)
            products = [i for i in heads if not (by_scalar and i == G - 1)]
            for i in heads[:2]:
                scores_matmul(ahead, i, i + 1)
            if turned:
                turn_back(k)
            scores_matmul(ahead, heads[2], heads[2] + 1)
            for i in products[:2]:
                weigh_scores(ahead, i, i + 1)
            scores_matmul(ahead, heads[3], heads[3] + 1)
            if turned:
                row_maxima(k, 3)
            if by_scalar:
                weigh_part(ahead)
            for i in products[2:]:
                weigh_scores(ahead, i, i + 1)
            run(values_matmul, k - 2)
            run(turn_queries, k + 3)
            exponentials(k)
            turn_e(k)
            if k + 3 < KV:
                copy_keys(k + 3)
            run(copy_queries, k + 3)
            if by_scalar:
                take_scores(ahead)
            run(normalise, k - 2)
            run(store, k - 2)
            group_e(k)
            if ahead == NG - 1:
                add_bias(ahead, 0, 2)
            elif lead:
                add_bias(ahead, 0, 3)
            else:
                add_bias(ahead)
            if by_scalar:
                weigh_taken(ahead)
            if k == 0:
                nc.vector.quantize_mx(
                    out=v_codes[:].bitcast(FP8X4), scales=v_scales[:],
                    in_=v_grouped[:].rearrange("p c t -> p (c t)"),
                )
        y, z = NG - 2, NG - 1
        quantise_e(y - 2)
        invert_sums(y - 2)
        values_matmul(y - 2)
        turn_back(z)
        row_maxima(y)
        exponentials(y)
        turn_e(y)
        normalise(y - 2)
        store(y - 2)
        add_bias(z, 2, 3)
        row_maxima(z, 0, 2)
        exponentials(z, 0, 2)
        quantise_e(y - 1)
        invert_sums(y - 1)
        values_matmul(y - 1)
        row_maxima(z, 3)
        group_e(y, 0, 2, eng="V")
        turn_e(z, 0, 2)
        exponentials(z, 3)
        turn_e(z, 3, spare=True)
        row_maxima(z, 2, 3)
        group_e(y, 2, eng="V")
        normalise(y - 1)
        store(y - 1)
        exponentials(z, 2, 3)
        turn_e(z, 2, 3, spare=True)
        quantise_e(y)
        invert_sums(y)
        values_matmul(y, spare=True)
        group_e(z, 3)
        group_e(z, 0, 2, eng="V")
        quantise_e(z, 0, 2)
        group_e(z, 2, 3)
        invert_sums(z)
        values_matmul(z, 0, 2, spare=True)
        quantise_e(z, 3)
        values_matmul(z, 3, spare=True)
        quantise_e(z, 2, 3)
        values_matmul(z, 2, 3, spare=True)
        normalise(y)
        store(y)
        normalise(z, 0, 2, eng="V")
        store(z, 0, 2)
        normalise(z, 3)
        store(z, 3, queue=nc.scalar)
        normalise(z, 2, 3, eng="V")
        store(z, 2, 3)
